import numpy as np
import ml_dtypes


def mxq(x, axis, fmt="e4m3"):
    dtype, down = {"e4m3": (ml_dtypes.float8_e4m3fn, 7), "e5m2": (ml_dtypes.float8_e5m2, 14)}[fmt]
    v = np.moveaxis(np.asarray(x, np.float32).astype(ml_dtypes.bfloat16).astype(np.float64), axis, -1)
    blocks = v.reshape(v.shape[:-1] + (-1, 32))
    amax = np.abs(blocks).max(-1, keepdims=True)
    byte = np.maximum(np.where(amax > 0, np.frexp(amax)[1] - 1 + 127, 0) - down, 1)
    scale = np.exp2(byte - 127.0)
    codes = (blocks / scale).astype(np.float32).astype(dtype).astype(np.float64)
    return np.moveaxis((codes * scale).reshape(v.shape), -1, axis)


WIDE = False


def mx_kscale(k):
    if not WIDE:
        return np.ones(k)
    levels = np.array([10, -10, 5, -5, 0])
    a = np.random.permutation(np.resize(levels, k // 512 * 4)).reshape(k // 512, 4)
    idx = np.arange(k)
    return np.exp2(a[idx // 512, idx % 128 // 32])


BF16 = ml_dtypes.bfloat16


def bf(x):
    return np.asarray(x, np.float32).astype(BF16)


def f64(x):
    return np.asarray(x).astype(np.float64)


B, S, D, H, HD, P = 4, 256, 512, 2, 128, 512
N = H * HD
THETA = 500000.0


def rope(t, cos, sin):
    tr = t[..., 0::2]
    ti = t[..., 1::2]
    c = cos[None, :, None, :]
    s = sin[None, :, None, :]
    out = np.stack([tr * c - ti * s, tr * s + ti * c], axis=-1)
    return out.reshape(t.shape)


def setup_inputs():
    s = mx_kscale(D)
    inv = 1.0 / THETA ** (np.arange(0, HD, 2) / HD)
    ang = np.outer(np.arange(S), inv)
    return {"x": bf(np.random.standard_normal((B, S, D)) * s),
            "wq": bf(np.random.standard_normal((N, D)) / np.sqrt(D) / s[None, :]),
            "wk": bf(np.random.standard_normal((N, D)) / np.sqrt(D) / s[None, :]),
            "freqs_cos": bf(np.cos(ang)),
            "freqs_sin": bf(np.sin(ang))}


def reference(x, wq, wk, freqs_cos, freqs_sin):
    xm = mxq(f64(x), 2, "e4m3")
    xq = (xm @ mxq(f64(wq), 1, "e4m3").T).reshape(B, S, H, HD)
    xk = (xm @ mxq(f64(wk), 1, "e4m3").T).reshape(B, S, H, HD)
    q = rope(xq, f64(freqs_cos), f64(freqs_sin)).transpose(0, 2, 1, 3)
    k = rope(xk, f64(freqs_cos), f64(freqs_sin)).transpose(0, 2, 1, 3)
    return q, k

@@ -1,0 +1,129 @@
+import concourse.mybir as mybir
+from concourse.masks import make_identity
+
+BF16 = mybir.dt.bfloat16
+F32 = mybir.dt.float32
+U32 = mybir.dt.uint32
+U8 = mybir.dt.uint8
+FP8X4 = mybir.dt.float8_e4m3fn_x4
+MULT = mybir.AluOpType.mult
+ADD = mybir.AluOpType.add
+
+P = 128
+BATCH = 4
+SEQ = 256
+K = 512
+PACK = 4
+HALVES = 2
+HEADS = 2
+HEAD_DIM = 128
+FREQS = HEAD_DIM // 2
+POS = SEQ // P
+PAIR = 2
+MATS = 2
+GROUPS = MATS * HEADS
+
+FLOPS = 2 * BATCH * SEQ * K * MATS * HEADS * HEAD_DIM
+
+
+def transpose_and_group(nc, banks, identity, rows, grouped, copy):
+    flipped = banks.tile([P, 2, HALVES, P], F32, tag="flipped")
+    for s in range(2):
+        words = rows[:, s, :].bitcast(F32)
+        for u in range(HALVES):
+            nc.tensor.transpose(flipped[:, s, u, :], words[:, u * P : (u + 1) * P], identity)
+    copy(out=grouped, in_=flipped[:].rearrange("p s u r -> p s r u"))
+
+
+def tile_attention_pa_s_kernel(tc, x, wq, wk, freqs_cos, freqs_sin, out_0, out_1):
+    nc = tc.nc
+    with (
+        tc.tile_pool(name="keep", bufs=1) as keep,
+        tc.tile_pool(name="work", bufs=2) as work,
+        tc.psum_pool(name="flip_banks", bufs=4) as flip_banks,
+        tc.psum_pool(name="product_banks", bufs=2) as product_banks,
+    ):
+        w_rows = keep.tile([P, MATS, PAIR, K], BF16)
+        nc.sync.dma_start(out=w_rows[:, 0], in_=wq.rearrange("(n e) k -> n e k", e=PAIR))
+        nc.sync.dma_start(out=w_rows[:, 1], in_=wk.rearrange("(n e) k -> n e k", e=PAIR))
+        x_rows = keep.tile([P, BATCH, POS, K], BF16)
+        nc.sync.dma_start(out=x_rows[:, 0], in_=x[0].rearrange("(p t) k -> p t k", t=POS))
+        cos = keep.tile([P, POS, FREQS], BF16)
+        sin = keep.tile([P, POS, FREQS], BF16)
+        nc.sync.dma_start(out=cos[:], in_=freqs_cos.rearrange("(p t) i -> p t i", t=POS))
+        nc.sync.dma_start(out=sin[:], in_=freqs_sin.rearrange("(p t) i -> p t i", t=POS))
+        for b in range(1, BATCH):
+            nc.sync.dma_start(out=x_rows[:, b], in_=x[b].rearrange("(p t) k -> p t k", t=POS))
+
+        identity = keep.tile([P, P], F32)
+        make_identity(nc, identity[:])
+        minus_sin = keep.tile([P, POS, FREQS], BF16)
+        nc.vector.tensor_scalar_mul(out=minus_sin[:], in0=sin[:], scalar1=-1.0)
+
+        w_grouped = keep.tile([P, PAIR, MATS, P, PACK], BF16, align_bytes=64)
+        w_codes = keep.tile([P, PAIR, MATS * P], U32, align_bytes=64)
+        w_scales = keep.tile([P, PAIR, MATS * P], U8, align_bytes=64)
+        w_grouped_words = w_grouped[:].bitcast(F32)
+        transpose_and_group(
+            nc, flip_banks, identity[:], w_rows[:, 0], w_grouped_words[:, :, 0], nc.scalar.copy
+        )
+        transpose_and_group(
+            nc, flip_banks, identity[:], w_rows[:, 1], w_grouped_words[:, :, 1], nc.vector.tensor_copy
+        )
+        nc.vector.quantize_mx(
+            out=w_codes[:].rearrange("p e c -> p (e c)").bitcast(FP8X4),
+            scales=w_scales[:].rearrange("p e c -> p (e c)"),
+            in_=w_grouped[:].rearrange("p e m n j -> p (e m n j)"),
+        )
+
+        x_codes = keep.tile([P, BATCH, POS * P], U32, align_bytes=64)
+        x_scales = keep.tile([P, BATCH, POS * P], U8, align_bytes=64)
+        for b in range(BATCH):
+            x_grouped = keep.tile([P, POS, P, PACK], BF16, align_bytes=64, name="x_grouped%d" % b)
+            transpose_and_group(
+                nc, flip_banks, identity[:], x_rows[:, b], x_grouped[:].bitcast(F32), nc.scalar.copy
+            )
+            nc.vector.quantize_mx(
+                out=x_codes[:, b, :].bitcast(FP8X4),
+                scales=x_scales[:, b, :],
+                in_=x_grouped[:].rearrange("p t r j -> p (t r j)"),
+            )
+
+        table_shape = [P, POS, GROUPS, FREQS]
+        cos_all = cos[:].unsqueeze(2).to_broadcast(table_shape)
+        sin_all = sin[:].unsqueeze(2).to_broadcast(table_shape)
+        minus_sin_all = minus_sin[:].unsqueeze(2).to_broadcast(table_shape)
+        for b in range(BATCH):
+            members = []
+            for e in range(PAIR):
+                bank = product_banks.tile([P, POS, GROUPS, FREQS], F32, tag="member%d" % e)
+                for t in range(POS):
+                    nc.tensor.matmul_mx(
+                        out=bank[:, t].rearrange("p g i -> p (g i)"),
+                        lhsT=x_codes[:, b, t * P : (t + 1) * P].bitcast(FP8X4),
+                        lhsT_scale=x_scales[:, b, t * P : (t + 1) * P],
+                        rhs=w_codes[:, e, :].bitcast(FP8X4),
+                        rhs_scale=w_scales[:, e, :],
+                        start=True,
+                        stop=True,
+                    )
+                members.append(bank)
+            even, odd = members
+            by_cos = work.tile([P, PAIR, POS, GROUPS, FREQS], F32)
+            by_sin = work.tile([P, PAIR, POS, GROUPS, FREQS], F32)
+            nc.vector.tensor_tensor(out=by_cos[:, 0], in0=even[:], in1=cos_all, op=MULT)
+            nc.vector.tensor_tensor(out=by_sin[:, 0], in0=odd[:], in1=minus_sin_all, op=MULT)
+            nc.vector.tensor_tensor(out=by_cos[:, 1], in0=odd[:], in1=cos_all, op=MULT)
+            nc.vector.tensor_tensor(out=by_sin[:, 1], in0=even[:], in1=sin_all, op=MULT)
+            rotated = work.tile([P, GROUPS, POS, FREQS, PAIR], F32)
+            nc.gpsimd.tensor_tensor(
+                out=rotated[:].rearrange("p g t i e -> p t g i e"),
+                in0=by_cos[:].rearrange("p e t g i -> p t g i e"),
+                in1=by_sin[:].rearrange("p e t g i -> p t g i e"),
+                op=ADD,
+            )
+            for m, result in enumerate((out_0, out_1)):
+                nc.sync.dma_start(
+                    out=result[b].rearrange("h (p t) d -> p h (t d)", t=POS),
+                    in_=rotated[:, m * HEADS : (m + 1) * HEADS].rearrange("p h t i e -> p h (t i e)"),
+                )

@@ -22,6 +22,7 @@ POS = SEQ // P
 PAIR = 2
 MATS = 2
 GROUPS = MATS * HEADS
+GPSIMD_BATCHES = 2
 
 FLOPS = 2 * BATCH * SEQ * K * MATS * HEADS * HEAD_DIM
 
@@ -39,7 +40,7 @@ def tile_attention_pa_s_kernel(tc, x, wq, wk, freqs_cos, freqs_sin, out_0, out_1
     nc = tc.nc
     with (
         tc.tile_pool(name="keep", bufs=1) as keep,
-        tc.tile_pool(name="work", bufs=2) as work,
+        tc.tile_pool(name="work", bufs=BATCH) as work,
         tc.psum_pool(name="flip_banks", bufs=4) as flip_banks,
         tc.psum_pool(name="product_banks", bufs=2) as product_banks,
     ):
@@ -47,18 +48,15 @@ def tile_attention_pa_s_kernel(tc, x, wq, wk, freqs_cos, freqs_sin, out_0, out_1
         nc.sync.dma_start(out=w_rows[:, 0], in_=wq.rearrange("(n e) k -> n e k", e=PAIR))
         nc.sync.dma_start(out=w_rows[:, 1], in_=wk.rearrange("(n e) k -> n e k", e=PAIR))
         x_rows = keep.tile([P, BATCH, POS, K], BF16)
-        nc.sync.dma_start(out=x_rows[:, 0], in_=x[0].rearrange("(p t) k -> p t k", t=POS))
+        for b in range(BATCH):
+            nc.sync.dma_start(out=x_rows[:, b], in_=x[b].rearrange("(p t) k -> p t k", t=POS))
         cos = keep.tile([P, POS, FREQS], BF16)
         sin = keep.tile([P, POS, FREQS], BF16)
-        nc.sync.dma_start(out=cos[:], in_=freqs_cos.rearrange("(p t) i -> p t i", t=POS))
-        nc.sync.dma_start(out=sin[:], in_=freqs_sin.rearrange("(p t) i -> p t i", t=POS))
-        for b in range(1, BATCH):
-            nc.sync.dma_start(out=x_rows[:, b], in_=x[b].rearrange("(p t) k -> p t k", t=POS))
+        nc.scalar.dma_start(out=cos[:], in_=freqs_cos.rearrange("(p t) i -> p t i", t=POS))
+        nc.scalar.dma_start(out=sin[:], in_=freqs_sin.rearrange("(p t) i -> p t i", t=POS))
 
         identity = keep.tile([P, P], F32)
         make_identity(nc, identity[:])
-        minus_sin = keep.tile([P, POS, FREQS], BF16)
-        nc.vector.tensor_scalar_mul(out=minus_sin[:], in0=sin[:], scalar1=-1.0)
 
         w_grouped = keep.tile([P, PAIR, MATS, P, PACK], BF16, align_bytes=64)
         w_codes = keep.tile([P, PAIR, MATS * P], U32, align_bytes=64)
@@ -81,7 +79,12 @@ def tile_attention_pa_s_kernel(tc, x, wq, wk, freqs_cos, freqs_sin, out_0, out_1
         for b in range(BATCH):
             x_grouped = keep.tile([P, POS, P, PACK], BF16, align_bytes=64, name="x_grouped%d" % b)
             transpose_and_group(
-                nc, flip_banks, identity[:], x_rows[:, b], x_grouped[:].bitcast(F32), nc.scalar.copy
+                nc,
+                flip_banks,
+                identity[:],
+                x_rows[:, b],
+                x_grouped[:].bitcast(F32),
+                nc.scalar.copy if b % 2 == 0 else nc.vector.tensor_copy,
             )
             nc.vector.quantize_mx(
                 out=x_codes[:, b, :].bitcast(FP8X4),
@@ -89,6 +92,8 @@ def tile_attention_pa_s_kernel(tc, x, wq, wk, freqs_cos, freqs_sin, out_0, out_1
                 in_=x_grouped[:].rearrange("p t r j -> p (t r j)"),
             )
 
+        minus_sin = keep.tile([P, POS, FREQS], BF16)
+        nc.vector.tensor_scalar_mul(out=minus_sin[:], in0=sin[:], scalar1=-1.0)
         table_shape = [P, POS, GROUPS, FREQS]
         cos_all = cos[:].unsqueeze(2).to_broadcast(table_shape)
         sin_all = sin[:].unsqueeze(2).to_broadcast(table_shape)
@@ -115,15 +120,17 @@ def tile_attention_pa_s_kernel(tc, x, wq, wk, freqs_cos, freqs_sin, out_0, out_1
             nc.vector.tensor_tensor(out=by_sin[:, 0], in0=odd[:], in1=minus_sin_all, op=MULT)
             nc.vector.tensor_tensor(out=by_cos[:, 1], in0=odd[:], in1=cos_all, op=MULT)
             nc.vector.tensor_tensor(out=by_sin[:, 1], in0=even[:], in1=sin_all, op=MULT)
+            adder = nc.gpsimd if b < GPSIMD_BATCHES else nc.vector
             rotated = work.tile([P, GROUPS, POS, FREQS, PAIR], F32)
-            nc.gpsimd.tensor_tensor(
-                out=rotated[:].rearrange("p g t i e -> p t g i e"),
-                in0=by_cos[:].rearrange("p e t g i -> p t g i e"),
-                in1=by_sin[:].rearrange("p e t g i -> p t g i e"),
-                op=ADD,
-            )
             for m, result in enumerate((out_0, out_1)):
+                heads = slice(m * HEADS, (m + 1) * HEADS)
+                adder.tensor_tensor(
+                    out=rotated[:, heads].rearrange("p h t i e -> p t h i e"),
+                    in0=by_cos[:, :, :, heads].rearrange("p e t h i -> p t h i e"),
+                    in1=by_sin[:, :, :, heads].rearrange("p e t h i -> p t h i e"),
+                    op=ADD,
+                )
                 nc.sync.dma_start(
                     out=result[b].rearrange("h (p t) d -> p h (t d)", t=POS),
-                    in_=rotated[:, m * HEADS : (m + 1) * HEADS].rearrange("p h t i e -> p h (t i e)"),
+                    in_=rotated[:, heads].rearrange("p h t i e -> p h (t i e)"),
                 )

@@ -8,6 +8,7 @@ U8 = mybir.dt.uint8
 FP8X4 = mybir.dt.float8_e4m3fn_x4
 MULT = mybir.AluOpType.mult
 ADD = mybir.AluOpType.add
+SUBTRACT = mybir.AluOpType.subtract
 
 P = 128
 BATCH = 4
@@ -22,7 +23,7 @@ POS = SEQ // P
 PAIR = 2
 MATS = 2
 GROUPS = MATS * HEADS
-GPSIMD_BATCHES = 2
+GPSIMD_SUMS = 5
 
 FLOPS = 2 * BATCH * SEQ * K * MATS * HEADS * HEAD_DIM
 
@@ -41,7 +42,7 @@ def tile_attention_pa_s_kernel(tc, x, wq, wk, freqs_cos, freqs_sin, out_0, out_1
     with (
         tc.tile_pool(name="keep", bufs=1) as keep,
         tc.tile_pool(name="work", bufs=BATCH) as work,
-        tc.psum_pool(name="flip_banks", bufs=4) as flip_banks,
+        tc.psum_pool(name="flip_banks", bufs=2) as flip_banks,
         tc.psum_pool(name="product_banks", bufs=2) as product_banks,
     ):
         w_rows = keep.tile([P, MATS, PAIR, K], BF16)
@@ -57,6 +58,14 @@ def tile_attention_pa_s_kernel(tc, x, wq, wk, freqs_cos, freqs_sin, out_0, out_1
 
         identity = keep.tile([P, P], F32)
         make_identity(nc, identity[:])
+        minus_cos = keep.tile([P, POS, FREQS], F32)
+        minus_cos_minus_sin = keep.tile([P, POS, FREQS], F32)
+        sin_minus_cos = keep.tile([P, POS, FREQS], F32)
+        nc.gpsimd.tensor_scalar(
+            out=minus_cos[:], in0=cos[:], scalar1=-1.0, scalar2=0.0, op0=MULT, op1=ADD
+        )
+        nc.gpsimd.tensor_tensor(out=minus_cos_minus_sin[:], in0=minus_cos[:], in1=sin[:], op=SUBTRACT)
+        nc.gpsimd.tensor_tensor(out=sin_minus_cos[:], in0=sin[:], in1=cos[:], op=SUBTRACT)
 
         w_grouped = keep.tile([P, PAIR, MATS, P, PACK], BF16, align_bytes=64)
         w_codes = keep.tile([P, PAIR, MATS * P], U32, align_bytes=64)
@@ -79,12 +88,7 @@ def tile_attention_pa_s_kernel(tc, x, wq, wk, freqs_cos, freqs_sin, out_0, out_1
         for b in range(BATCH):
             x_grouped = keep.tile([P, POS, P, PACK], BF16, align_bytes=64, name="x_grouped%d" % b)
             transpose_and_group(
-                nc,
-                flip_banks,
-                identity[:],
-                x_rows[:, b],
-                x_grouped[:].bitcast(F32),
-                nc.scalar.copy if b % 2 == 0 else nc.vector.tensor_copy,
+                nc, flip_banks, identity[:], x_rows[:, b], x_grouped[:].bitcast(F32), nc.scalar.copy
             )
             nc.vector.quantize_mx(
                 out=x_codes[:, b, :].bitcast(FP8X4),
@@ -92,45 +96,52 @@ def tile_attention_pa_s_kernel(tc, x, wq, wk, freqs_cos, freqs_sin, out_0, out_1
                 in_=x_grouped[:].rearrange("p t r j -> p (t r j)"),
             )
 
-        minus_sin = keep.tile([P, POS, FREQS], BF16)
-        nc.vector.tensor_scalar_mul(out=minus_sin[:], in0=sin[:], scalar1=-1.0)
-        table_shape = [P, POS, GROUPS, FREQS]
-        cos_all = cos[:].unsqueeze(2).to_broadcast(table_shape)
-        sin_all = sin[:].unsqueeze(2).to_broadcast(table_shape)
-        minus_sin_all = minus_sin[:].unsqueeze(2).to_broadcast(table_shape)
-        for b in range(BATCH):
-            members = []
-            for e in range(PAIR):
-                bank = product_banks.tile([P, POS, GROUPS, FREQS], F32, tag="member%d" % e)
-                for t in range(POS):
+        def for_all_groups(table):
+            return table[:].unsqueeze(2).to_broadcast([P, POS, GROUPS, FREQS])
+
+        def project(bank, b, members):
+            for t in range(POS):
+                for e in members:
                     nc.tensor.matmul_mx(
                         out=bank[:, t].rearrange("p g i -> p (g i)"),
                         lhsT=x_codes[:, b, t * P : (t + 1) * P].bitcast(FP8X4),
                         lhsT_scale=x_scales[:, b, t * P : (t + 1) * P],
                         rhs=w_codes[:, e, :].bitcast(FP8X4),
                         rhs_scale=w_scales[:, e, :],
-                        start=True,
-                        stop=True,
+                        start=(e == members[0]),
+                        stop=(e == members[-1]),
                     )
-                members.append(bank)
-            even, odd = members
-            by_cos = work.tile([P, PAIR, POS, GROUPS, FREQS], F32)
-            by_sin = work.tile([P, PAIR, POS, GROUPS, FREQS], F32)
-            nc.vector.tensor_tensor(out=by_cos[:, 0], in0=even[:], in1=cos_all, op=MULT)
-            nc.vector.tensor_tensor(out=by_sin[:, 0], in0=odd[:], in1=minus_sin_all, op=MULT)
-            nc.vector.tensor_tensor(out=by_cos[:, 1], in0=odd[:], in1=cos_all, op=MULT)
-            nc.vector.tensor_tensor(out=by_sin[:, 1], in0=even[:], in1=sin_all, op=MULT)
-            adder = nc.gpsimd if b < GPSIMD_BATCHES else nc.vector
+
+        for b in range(BATCH):
+            even = product_banks.tile([P, POS, GROUPS, FREQS], F32)
+            odd = product_banks.tile([P, POS, GROUPS, FREQS], F32)
+            both = product_banks.tile([P, POS, GROUPS, FREQS], F32)
+            project(even, b, (0,))
+            project(odd, b, (1,))
+            project(both, b, (0, 1))
+            own = work.tile([P, PAIR, POS, GROUPS, FREQS], F32)
+            shared = work.tile([P, POS, GROUPS, FREQS], F32)
+            nc.vector.tensor_tensor(
+                out=own[:, 1], in0=even[:], in1=for_all_groups(sin_minus_cos), op=MULT
+            )
+            nc.vector.tensor_tensor(
+                out=own[:, 0], in0=odd[:], in1=for_all_groups(minus_cos_minus_sin), op=MULT
+            )
+            nc.vector.tensor_tensor(out=shared[:], in0=both[:], in1=for_all_groups(cos), op=MULT)
             rotated = work.tile([P, GROUPS, POS, FREQS, PAIR], F32)
             for m, result in enumerate((out_0, out_1)):
                 heads = slice(m * HEADS, (m + 1) * HEADS)
+                if MATS * b + m < GPSIMD_SUMS:
+                    adder, store_queue = nc.gpsimd, nc.scalar
+                else:
+                    adder, store_queue = nc.vector, nc.sync
                 adder.tensor_tensor(
                     out=rotated[:, heads].rearrange("p h t i e -> p t h i e"),
-                    in0=by_cos[:, :, :, heads].rearrange("p e t h i -> p t h i e"),
-                    in1=by_sin[:, :, :, heads].rearrange("p e t h i -> p t h i e"),
+                    in0=shared[:, :, heads].unsqueeze(4).to_broadcast([P, POS, HEADS, FREQS, PAIR]),
+                    in1=own[:, :, :, heads].rearrange("p e t h i -> p t h i e"),
                     op=ADD,
                 )
-                nc.sync.dma_start(
+                store_queue.dma_start(
                     out=result[b].rearrange("h (p t) d -> p h (t d)", t=POS),
                     in_=rotated[:, heads].rearrange("p h t i e -> p h (t i e)"),
                 )

@@ -24,12 +24,13 @@ PAIR = 2
 MATS = 2
 GROUPS = MATS * HEADS
 GPSIMD_SUMS = 5
+PSUM_BANKS = 8
 
 FLOPS = 2 * BATCH * SEQ * K * MATS * HEADS * HEAD_DIM
 
 
 def transpose_and_group(nc, banks, identity, rows, grouped, copy):
-    flipped = banks.tile([P, 2, HALVES, P], F32, tag="flipped")
+    flipped = banks.tile([P, 2, HALVES, P], F32, tag="bank")
     for s in range(2):
         words = rows[:, s, :].bitcast(F32)
         for u in range(HALVES):
@@ -42,8 +43,7 @@ def tile_attention_pa_s_kernel(tc, x, wq, wk, freqs_cos, freqs_sin, out_0, out_1
     with (
         tc.tile_pool(name="keep", bufs=1) as keep,
         tc.tile_pool(name="work", bufs=BATCH) as work,
-        tc.psum_pool(name="flip_banks", bufs=2) as flip_banks,
-        tc.psum_pool(name="product_banks", bufs=2) as product_banks,
+        tc.psum_pool(name="banks", bufs=PSUM_BANKS) as banks,
     ):
         w_rows = keep.tile([P, MATS, PAIR, K], BF16)
         nc.sync.dma_start(out=w_rows[:, 0], in_=wq.rearrange("(n e) k -> n e k", e=PAIR))
@@ -72,10 +72,10 @@ def tile_attention_pa_s_kernel(tc, x, wq, wk, freqs_cos, freqs_sin, out_0, out_1
         w_scales = keep.tile([P, PAIR, MATS * P], U8, align_bytes=64)
         w_grouped_words = w_grouped[:].bitcast(F32)
         transpose_and_group(
-            nc, flip_banks, identity[:], w_rows[:, 0], w_grouped_words[:, :, 0], nc.scalar.copy
+            nc, banks, identity[:], w_rows[:, 0], w_grouped_words[:, :, 0], nc.scalar.copy
         )
         transpose_and_group(
-            nc, flip_banks, identity[:], w_rows[:, 1], w_grouped_words[:, :, 1], nc.vector.tensor_copy
+            nc, banks, identity[:], w_rows[:, 1], w_grouped_words[:, :, 1], nc.vector.tensor_copy
         )
         nc.vector.quantize_mx(
             out=w_codes[:].rearrange("p e c -> p (e c)").bitcast(FP8X4),
@@ -88,7 +88,12 @@ def tile_attention_pa_s_kernel(tc, x, wq, wk, freqs_cos, freqs_sin, out_0, out_1
         for b in range(BATCH):
             x_grouped = keep.tile([P, POS, P, PACK], BF16, align_bytes=64, name="x_grouped%d" % b)
             transpose_and_group(
-                nc, flip_banks, identity[:], x_rows[:, b], x_grouped[:].bitcast(F32), nc.scalar.copy
+                nc,
+                banks,
+                identity[:],
+                x_rows[:, b],
+                x_grouped[:].bitcast(F32),
+                nc.scalar.copy if b % 2 == 0 else nc.vector.tensor_copy,
             )
             nc.vector.quantize_mx(
                 out=x_codes[:, b, :].bitcast(FP8X4),
@@ -113,9 +118,9 @@ def tile_attention_pa_s_kernel(tc, x, wq, wk, freqs_cos, freqs_sin, out_0, out_1
                     )
 
         for b in range(BATCH):
-            even = product_banks.tile([P, POS, GROUPS, FREQS], F32)
-            odd = product_banks.tile([P, POS, GROUPS, FREQS], F32)
-            both = product_banks.tile([P, POS, GROUPS, FREQS], F32)
+            even = banks.tile([P, POS, GROUPS, FREQS], F32, tag="bank")
+            odd = banks.tile([P, POS, GROUPS, FREQS], F32, tag="bank")
+            both = banks.tile([P, POS, GROUPS, FREQS], F32, tag="bank")
             project(even, b, (0,))
             project(odd, b, (1,))
             project(both, b, (0, 1))

@@ -23,7 +23,7 @@ POS = SEQ // P
 PAIR = 2
 MATS = 2
 GROUPS = MATS * HEADS
-GPSIMD_SUMS = 5
+GPSIMD_SUMS = 4
 PSUM_BANKS = 8
 
 FLOPS = 2 * BATCH * SEQ * K * MATS * HEADS * HEAD_DIM

@@ -23,19 +23,12 @@ POS = SEQ // P
 PAIR = 2
 MATS = 2
 GROUPS = MATS * HEADS
+TERM_MEMBERS = ((0,), (1,), (0, 1))
+TERMS = len(TERM_MEMBERS)
 GPSIMD_SUMS = 4
 PSUM_BANKS = 8
 
 FLOPS = 2 * BATCH * SEQ * K * MATS * HEADS * HEAD_DIM
-
-
-def transpose_and_group(nc, banks, identity, rows, grouped, copy):
-    flipped = banks.tile([P, 2, HALVES, P], F32, tag="bank")
-    for s in range(2):
-        words = rows[:, s, :].bitcast(F32)
-        for u in range(HALVES):
-            nc.tensor.transpose(flipped[:, s, u, :], words[:, u * P : (u + 1) * P], identity)
-    copy(out=grouped, in_=flipped[:].rearrange("p s u r -> p s r u"))
 
 
 def tile_attention_pa_s_kernel(tc, x, wq, wk, freqs_cos, freqs_sin, out_0, out_1):
@@ -44,6 +37,7 @@ def tile_attention_pa_s_kernel(tc, x, wq, wk, freqs_cos, freqs_sin, out_0, out_1
         tc.tile_pool(name="keep", bufs=1) as keep,
         tc.tile_pool(name="work", bufs=BATCH) as work,
         tc.psum_pool(name="banks", bufs=PSUM_BANKS) as banks,
+        tc.manual_schedule(),
     ):
         w_rows = keep.tile([P, MATS, PAIR, K], BF16)
         nc.sync.dma_start(out=w_rows[:, 0], in_=wq.rearrange("(n e) k -> n e k", e=PAIR))
@@ -66,73 +60,70 @@ def tile_attention_pa_s_kernel(tc, x, wq, wk, freqs_cos, freqs_sin, out_0, out_1
         )
         nc.gpsimd.tensor_tensor(out=minus_cos_minus_sin[:], in0=minus_cos[:], in1=sin[:], op=SUBTRACT)
         nc.gpsimd.tensor_tensor(out=sin_minus_cos[:], in0=sin[:], in1=cos[:], op=SUBTRACT)
+        term_factors = (sin_minus_cos, minus_cos_minus_sin, cos)
+
+        def transpose_and_group(rows, grouped, copy):
+            flipped = banks.tile([P, 2, HALVES, P], F32, tag="bank")
+            for s in range(2):
+                words = rows[:, s, :].bitcast(F32)
+                for u in range(HALVES):
+                    nc.tensor.transpose(
+                        flipped[:, s, u, :], words[:, u * P : (u + 1) * P], identity[:]
+                    )
+            copy(out=grouped, in_=flipped[:].rearrange("p s u r -> p s r u"))
 
         w_grouped = keep.tile([P, PAIR, MATS, P, PACK], BF16, align_bytes=64)
+        w_grouped_words = w_grouped[:].bitcast(F32)
+        transpose_and_group(w_rows[:, 0], w_grouped_words[:, :, 0], nc.scalar.copy)
+        transpose_and_group(w_rows[:, 1], w_grouped_words[:, :, 1], nc.vector.tensor_copy)
+        x_grouped = keep.tile([P, BATCH, POS, P, PACK], BF16, align_bytes=64)
+        for b in range(BATCH):
+            transpose_and_group(x_rows[:, b], x_grouped[:, b].bitcast(F32), nc.scalar.copy)
+
         w_codes = keep.tile([P, PAIR, MATS * P], U32, align_bytes=64)
         w_scales = keep.tile([P, PAIR, MATS * P], U8, align_bytes=64)
-        w_grouped_words = w_grouped[:].bitcast(F32)
-        transpose_and_group(
-            nc, banks, identity[:], w_rows[:, 0], w_grouped_words[:, :, 0], nc.scalar.copy
-        )
-        transpose_and_group(
-            nc, banks, identity[:], w_rows[:, 1], w_grouped_words[:, :, 1], nc.vector.tensor_copy
-        )
-        nc.vector.quantize_mx(
-            out=w_codes[:].rearrange("p e c -> p (e c)").bitcast(FP8X4),
-            scales=w_scales[:].rearrange("p e c -> p (e c)"),
-            in_=w_grouped[:].rearrange("p e m n j -> p (e m n j)"),
-        )
-
         x_codes = keep.tile([P, BATCH, POS * P], U32, align_bytes=64)
         x_scales = keep.tile([P, BATCH, POS * P], U8, align_bytes=64)
-        for b in range(BATCH):
-            x_grouped = keep.tile([P, POS, P, PACK], BF16, align_bytes=64, name="x_grouped%d" % b)
-            transpose_and_group(
-                nc,
-                banks,
-                identity[:],
-                x_rows[:, b],
-                x_grouped[:].bitcast(F32),
-                nc.scalar.copy if b % 2 == 0 else nc.vector.tensor_copy,
-            )
+
+        def quantise_x(b):
             nc.vector.quantize_mx(
                 out=x_codes[:, b, :].bitcast(FP8X4),
                 scales=x_scales[:, b, :],
-                in_=x_grouped[:].rearrange("p t r j -> p (t r j)"),
+                in_=x_grouped[:, b].rearrange("p t r j -> p (t r j)"),
             )
 
-        def for_all_groups(table):
-            return table[:].unsqueeze(2).to_broadcast([P, POS, GROUPS, FREQS])
+        def project(b):
+            projected = []
+            for j, members in enumerate(TERM_MEMBERS):
+                bank = banks.tile([P, POS, GROUPS, FREQS], F32, tag="bank", name="projected%d" % j)
+                for t in range(POS):
+                    for e in members:
+                        nc.tensor.matmul_mx(
+                            out=bank[:, t].rearrange("p g i -> p (g i)"),
+                            lhsT=x_codes[:, b, t * P : (t + 1) * P].bitcast(FP8X4),
+                            lhsT_scale=x_scales[:, b, t * P : (t + 1) * P],
+                            rhs=w_codes[:, e, :].bitcast(FP8X4),
+                            rhs_scale=w_scales[:, e, :],
+                            start=(e == members[0]),
+                            stop=(e == members[-1]),
+                        )
+                projected.append(bank)
+            return projected
 
-        def project(bank, b, members):
-            for t in range(POS):
-                for e in members:
-                    nc.tensor.matmul_mx(
-                        out=bank[:, t].rearrange("p g i -> p (g i)"),
-                        lhsT=x_codes[:, b, t * P : (t + 1) * P].bitcast(FP8X4),
-                        lhsT_scale=x_scales[:, b, t * P : (t + 1) * P],
-                        rhs=w_codes[:, e, :].bitcast(FP8X4),
-                        rhs_scale=w_scales[:, e, :],
-                        start=(e == members[0]),
-                        stop=(e == members[-1]),
-                    )
-
-        for b in range(BATCH):
-            even = banks.tile([P, POS, GROUPS, FREQS], F32, tag="bank")
-            odd = banks.tile([P, POS, GROUPS, FREQS], F32, tag="bank")
-            both = banks.tile([P, POS, GROUPS, FREQS], F32, tag="bank")
-            project(even, b, (0,))
-            project(odd, b, (1,))
-            project(both, b, (0, 1))
+        def new_terms():
             own = work.tile([P, PAIR, POS, GROUPS, FREQS], F32)
             shared = work.tile([P, POS, GROUPS, FREQS], F32)
+            return own, shared
+
+        def form_term(j, projected, own, shared):
             nc.vector.tensor_tensor(
-                out=own[:, 1], in0=even[:], in1=for_all_groups(sin_minus_cos), op=MULT
+                out=(own[:, 1], own[:, 0], shared[:])[j],
+                in0=projected[j][:],
+                in1=term_factors[j][:].unsqueeze(2).to_broadcast([P, POS, GROUPS, FREQS]),
+                op=MULT,
             )
-            nc.vector.tensor_tensor(
-                out=own[:, 0], in0=odd[:], in1=for_all_groups(minus_cos_minus_sin), op=MULT
-            )
-            nc.vector.tensor_tensor(out=shared[:], in0=both[:], in1=for_all_groups(cos), op=MULT)
+
+        def sum_and_store(b, own, shared):
             rotated = work.tile([P, GROUPS, POS, FREQS, PAIR], F32)
             for m, result in enumerate((out_0, out_1)):
                 heads = slice(m * HEADS, (m + 1) * HEADS)
@@ -150,3 +141,24 @@ def tile_attention_pa_s_kernel(tc, x, wq, wk, freqs_cos, freqs_sin, out_0, out_1
                     out=result[b].rearrange("h (p t) d -> p h (t d)", t=POS),
                     in_=rotated[:, heads].rearrange("p h t i e -> p h (t i e)"),
                 )
+
+        nc.vector.quantize_mx(
+            out=w_codes[:].rearrange("p e c -> p (e c)").bitcast(FP8X4),
+            scales=w_scales[:].rearrange("p e c -> p (e c)"),
+            in_=w_grouped[:].rearrange("p e m n j -> p (e m n j)"),
+        )
+        quantise_x(0)
+        projected = project(0)
+        own, shared = new_terms()
+        assert BATCH - 1 == TERMS
+        for j in range(TERMS):
+            quantise_x(j + 1)
+            form_term(j, projected, own, shared)
+        sum_and_store(0, own, shared)
+
+        for b in range(1, BATCH):
+            projected = project(b)
+            own, shared = new_terms()
+            for j in range(TERMS):
+                form_term(j, projected, own, shared)
+            sum_and_store(b, own, shared)

import concourse.mybir as mybir
from concourse.masks import make_identity

BF16 = mybir.dt.bfloat16
F32 = mybir.dt.float32
U32 = mybir.dt.uint32
U8 = mybir.dt.uint8
FP8X4 = mybir.dt.float8_e4m3fn_x4
MULT = mybir.AluOpType.mult
ADD = mybir.AluOpType.add
SUBTRACT = mybir.AluOpType.subtract

P = 128
BATCH = 4
SEQ = 256
K = 512
PACK = 4
HALVES = 2
HEADS = 2
HEAD_DIM = 128
FREQS = HEAD_DIM // 2
POS = SEQ // P
PAIR = 2
MATS = 2
GROUPS = MATS * HEADS
TERM_MEMBERS = ((0,), (1,), (0, 1))
TERMS = len(TERM_MEMBERS)
GPSIMD_SUMS = 4
PSUM_BANKS = 8

FLOPS = 2 * BATCH * SEQ * K * MATS * HEADS * HEAD_DIM


def tile_attention_pa_s_kernel(tc, x, wq, wk, freqs_cos, freqs_sin, out_0, out_1):
    nc = tc.nc
    with (
        tc.tile_pool(name="keep", bufs=1) as keep,
        tc.tile_pool(name="work", bufs=BATCH) as work,
        tc.psum_pool(name="banks", bufs=PSUM_BANKS) as banks,
        tc.manual_schedule(),
    ):
        w_rows = keep.tile([P, MATS, PAIR, K], BF16)
        nc.sync.dma_start(out=w_rows[:, 0], in_=wq.rearrange("(n e) k -> n e k", e=PAIR))
        nc.sync.dma_start(out=w_rows[:, 1], in_=wk.rearrange("(n e) k -> n e k", e=PAIR))
        x_rows = keep.tile([P, BATCH, POS, K], BF16)
        for b in range(BATCH):
            nc.sync.dma_start(out=x_rows[:, b], in_=x[b].rearrange("(p t) k -> p t k", t=POS))
        cos = keep.tile([P, POS, FREQS], BF16)
        sin = keep.tile([P, POS, FREQS], BF16)
        nc.scalar.dma_start(out=cos[:], in_=freqs_cos.rearrange("(p t) i -> p t i", t=POS))
        nc.scalar.dma_start(out=sin[:], in_=freqs_sin.rearrange("(p t) i -> p t i", t=POS))

        identity = keep.tile([P, P], F32)
        make_identity(nc, identity[:])
        minus_cos = keep.tile([P, POS, FREQS], F32)
        minus_cos_minus_sin = keep.tile([P, POS, FREQS], F32)
        sin_minus_cos = keep.tile([P, POS, FREQS], F32)
        nc.gpsimd.tensor_scalar(
            out=minus_cos[:], in0=cos[:], scalar1=-1.0, scalar2=0.0, op0=MULT, op1=ADD
        )
        nc.gpsimd.tensor_tensor(out=minus_cos_minus_sin[:], in0=minus_cos[:], in1=sin[:], op=SUBTRACT)
        nc.gpsimd.tensor_tensor(out=sin_minus_cos[:], in0=sin[:], in1=cos[:], op=SUBTRACT)
        term_factors = (sin_minus_cos, minus_cos_minus_sin, cos)

        def transpose_and_group(rows, grouped, copy):
            flipped = banks.tile([P, 2, HALVES, P], F32, tag="bank")
            for s in range(2):
                words = rows[:, s, :].bitcast(F32)
                for u in range(HALVES):
                    nc.tensor.transpose(
                        flipped[:, s, u, :], words[:, u * P : (u + 1) * P], identity[:]
                    )
            copy(out=grouped, in_=flipped[:].rearrange("p s u r -> p s r u"))

        w_grouped = keep.tile([P, PAIR, MATS, P, PACK], BF16, align_bytes=64)
        w_grouped_words = w_grouped[:].bitcast(F32)
        transpose_and_group(w_rows[:, 0], w_grouped_words[:, :, 0], nc.scalar.copy)
        transpose_and_group(w_rows[:, 1], w_grouped_words[:, :, 1], nc.vector.tensor_copy)
        x_grouped = keep.tile([P, BATCH, POS, P, PACK], BF16, align_bytes=64)
        for b in range(BATCH):
            transpose_and_group(x_rows[:, b], x_grouped[:, b].bitcast(F32), nc.scalar.copy)

        w_codes = keep.tile([P, PAIR, MATS * P], U32, align_bytes=64)
        w_scales = keep.tile([P, PAIR, MATS * P], U8, align_bytes=64)
        x_codes = keep.tile([P, BATCH, POS * P], U32, align_bytes=64)
        x_scales = keep.tile([P, BATCH, POS * P], U8, align_bytes=64)

        def quantise_x(b):
            nc.vector.quantize_mx(
                out=x_codes[:, b, :].bitcast(FP8X4),
                scales=x_scales[:, b, :],
                in_=x_grouped[:, b].rearrange("p t r j -> p (t r j)"),
            )

        def project(b):
            projected = []
            for j, members in enumerate(TERM_MEMBERS):
                bank = banks.tile([P, POS, GROUPS, FREQS], F32, tag="bank", name="projected%d" % j)
                for t in range(POS):
                    for e in members:
                        nc.tensor.matmul_mx(
                            out=bank[:, t].rearrange("p g i -> p (g i)"),
                            lhsT=x_codes[:, b, t * P : (t + 1) * P].bitcast(FP8X4),
                            lhsT_scale=x_scales[:, b, t * P : (t + 1) * P],
                            rhs=w_codes[:, e, :].bitcast(FP8X4),
                            rhs_scale=w_scales[:, e, :],
                            start=(e == members[0]),
                            stop=(e == members[-1]),
                        )
                projected.append(bank)
            return projected

        def new_terms():
            own = work.tile([P, PAIR, POS, GROUPS, FREQS], F32)
            shared = work.tile([P, POS, GROUPS, FREQS], F32)
            return own, shared

        def form_term(j, projected, own, shared):
            nc.vector.tensor_tensor(
                out=(own[:, 1], own[:, 0], shared[:])[j],
                in0=projected[j][:],
                in1=term_factors[j][:].unsqueeze(2).to_broadcast([P, POS, GROUPS, FREQS]),
                op=MULT,
            )

        def sum_and_store(b, own, shared):
            rotated = work.tile([P, GROUPS, POS, FREQS, PAIR], F32)
            for m, result in enumerate((out_0, out_1)):
                heads = slice(m * HEADS, (m + 1) * HEADS)
                if MATS * b + m < GPSIMD_SUMS:
                    adder, store_queue = nc.gpsimd, nc.scalar
                else:
                    adder, store_queue = nc.vector, nc.sync
                adder.tensor_tensor(
                    out=rotated[:, heads].rearrange("p h t i e -> p t h i e"),
                    in0=shared[:, :, heads].unsqueeze(4).to_broadcast([P, POS, HEADS, FREQS, PAIR]),
                    in1=own[:, :, :, heads].rearrange("p e t h i -> p t h i e"),
                    op=ADD,
                )
                store_queue.dma_start(
                    out=result[b].rearrange("h (p t) d -> p h (t d)", t=POS),
                    in_=rotated[:, heads].rearrange("p h t i e -> p h (t i e)"),
                )

        nc.vector.quantize_mx(
            out=w_codes[:].rearrange("p e c -> p (e c)").bitcast(FP8X4),
            scales=w_scales[:].rearrange("p e c -> p (e c)"),
            in_=w_grouped[:].rearrange("p e m n j -> p (e m n j)"),
        )
        quantise_x(0)
        projected = project(0)
        own, shared = new_terms()
        assert BATCH - 1 == TERMS
        for j in range(TERMS):
            quantise_x(j + 1)
            form_term(j, projected, own, shared)
        sum_and_store(0, own, shared)

        for b in range(1, BATCH):
            projected = project(b)
            own, shared = new_terms()
            for j in range(TERMS):
                form_term(j, projected, own, shared)
            sum_and_store(b, own, shared)
